import numpy as np
import ml_dtypes


def mxq(x, axis, fmt="e4m3"):
    dtype, down = {"e4m3": (ml_dtypes.float8_e4m3fn, 7), "e5m2": (ml_dtypes.float8_e5m2, 14)}[fmt]
    v = np.moveaxis(np.asarray(x, np.float32).astype(ml_dtypes.bfloat16).astype(np.float64), axis, -1)
    blocks = v.reshape(v.shape[:-1] + (-1, 32))
    amax = np.abs(blocks).max(-1, keepdims=True)
    byte = np.maximum(np.where(amax > 0, np.frexp(amax)[1] - 1 + 127, 0) - down, 1)
    scale = np.exp2(byte - 127.0)
    codes = (blocks / scale).astype(np.float32).astype(dtype).astype(np.float64)
    return np.moveaxis((codes * scale).reshape(v.shape), -1, axis)


WIDE = False


def mx_kscale(k):
    if not WIDE:
        return np.ones(k)
    levels = np.array([10, -10, 5, -5, 0])
    a = np.random.permutation(np.resize(levels, k // 512 * 4)).reshape(k // 512, 4)
    idx = np.arange(k)
    return np.exp2(a[idx // 512, idx % 128 // 32])


BF16 = ml_dtypes.bfloat16


def bf(x):
    return np.asarray(x, np.float32).astype(BF16)


def f64(x):
    return np.asarray(x).astype(np.float64)


N, D_IN, HEADS, DPH = 512, 1024, 8, 16
EDGE_P = 0.01


def setup_inputs():
    s, t = mx_kscale(D_IN), mx_kscale(N)
    edges = (np.random.random((N, N)) < EDGE_P).astype(np.float64)
    a = (edges + 0.1 * np.random.standard_normal((N, N))) / np.sqrt(EDGE_P * N)
    return {"H": bf(np.random.standard_normal((N, D_IN)) * s / t[:, None]),
            "adj": bf(a * t),
            "W": bf(np.random.standard_normal((HEADS, D_IN, DPH)) / np.sqrt(D_IN) / s[:, None]),
            "b": bf(np.random.standard_normal((HEADS, DPH)) * 0.2)}


def reference(H, adj, W, b):
    H_ = mxq(f64(H), 1, "e4m3") @ mxq(f64(W), 1, "e4m3")
    out = (mxq(f64(adj), 1, "e4m3") @ mxq(H_, 1, "e4m3")) + f64(b)[:, None, :]
    return np.transpose(out, (1, 0, 2)).reshape(H.shape[0], HEADS * DPH)

@@ -1,0 +1,145 @@
+from contextlib import ExitStack
+
+import concourse.mybir as mybir
+from concourse.masks import make_identity
+
+BF16 = mybir.dt.bfloat16
+F32 = mybir.dt.float32
+U32 = mybir.dt.uint32
+U8 = mybir.dt.uint8
+FP8X4 = mybir.dt.float8_e4m3fn_x4
+
+P = 128
+PACK = 4
+K_PASS = P * PACK
+PAIR = 2
+WORDS = PACK // PAIR
+
+NODES, FEATURES, HEADS, HEAD_WIDTH = 512, 1024, 8, 16
+COLUMNS = HEADS * HEAD_WIDTH
+ROW_GROUPS = NODES // P
+FEATURE_PASSES = FEATURES // K_PASS
+SECTIONS = 2
+
+FLOPS = 2 * NODES * FEATURES * COLUMNS + 2 * NODES * NODES * COLUMNS
+
+
+def tile_graphlayer_s_kernel(tc, H, adj, W, b, out):
+    nc = tc.nc
+    with ExitStack() as ctx:
+        consts = ctx.enter_context(tc.tile_pool(name="consts", bufs=1))
+        loads = ctx.enter_context(tc.tile_pool(name="loads", bufs=6))
+        stage = ctx.enter_context(tc.tile_pool(name="stage", bufs=6))
+        operands = ctx.enter_context(tc.tile_pool(name="operands", bufs=6))
+        flipped_banks = ctx.enter_context(tc.psum_pool(name="flipped", bufs=6))
+        product_banks = ctx.enter_context(tc.psum_pool(name="products", bufs=1))
+
+        w_raw = consts.tile([P, HEADS * FEATURE_PASSES, PACK * HEAD_WIDTH], BF16)
+        nc.sync.dma_start(
+            out=w_raw[:],
+            in_=W.rearrange("h (g p j) d -> p (h g) (j d)", g=FEATURE_PASSES, j=PACK),
+        )
+        h_tiles = []
+        for m in range(ROW_GROUPS):
+            h_rows = loads.tile([P, SECTIONS * K_PASS], BF16, tag="rows")
+            nc.sync.dma_start(out=h_rows[:], in_=H.rearrange("(p m) k -> m p k", m=ROW_GROUPS)[m])
+            h_tiles.append(h_rows)
+        adj_tiles = []
+        for a in range(ROW_GROUPS // SECTIONS):
+            adj_rows = loads.tile([P, SECTIONS * K_PASS], BF16, tag="rows")
+            nc.sync.dma_start(
+                out=adj_rows[:],
+                in_=adj.rearrange("(p a s) n -> a p (s n)", a=ROW_GROUPS // SECTIONS, s=SECTIONS)[a],
+            )
+            adj_tiles.append(adj_rows)
+        bias = consts.tile([P, COLUMNS], BF16)
+        nc.scalar.dma_start(out=bias[:], in_=b.rearrange("h d -> (h d)").partition_broadcast(P))
+
+        identity = consts.tile([P, P], F32)
+        make_identity(nc, identity[:])
+
+        w_grouped = consts.tile([P, FEATURE_PASSES * COLUMNS * PACK], BF16, align_bytes=64)
+        for g in range(FEATURE_PASSES):
+            nc.vector.tensor_copy(
+                out=w_grouped[:].rearrange(
+                    "p (g h d j) -> p g h d j", g=FEATURE_PASSES, h=HEADS, j=PACK
+                )[:, g],
+                in_=w_raw[:].rearrange(
+                    "p (h g) (j d) -> p g h d j", g=FEATURE_PASSES, j=PACK
+                )[:, g],
+            )
+        w_codes = consts.tile([P, FEATURE_PASSES * COLUMNS], U32, align_bytes=64)
+        w_scales = consts.tile([P, FEATURE_PASSES * COLUMNS], U8, align_bytes=64)
+        nc.vector.quantize_mx(out=w_codes[:].bitcast(FP8X4), scales=w_scales[:], in_=w_grouped[:])
+
+        def quantise_transposed(rows):
+            words = rows[:].bitcast(F32).rearrange("r (s p u) -> r s p u", s=SECTIONS, u=WORDS)
+            flipped = flipped_banks.tile([P, SECTIONS, WORDS, P], F32)
+            for s in range(SECTIONS):
+                for u in range(WORDS):
+                    nc.tensor.transpose(flipped[:, s, u, :], words[:, s, :, u], identity[:])
+            grouped = stage.tile([P, SECTIONS * P * PACK], BF16, align_bytes=64)
+            nc.scalar.copy(
+                out=grouped[:].bitcast(F32).rearrange("p (s r u) -> p s r u", s=SECTIONS, u=WORDS),
+                in_=flipped[:].rearrange("p s u r -> p s r u"),
+            )
+            codes = operands.tile([P, SECTIONS * P], U32, align_bytes=64)
+            scales = operands.tile([P, SECTIONS * P], U8, align_bytes=64)
+            nc.vector.quantize_mx(out=codes[:].bitcast(FP8X4), scales=scales[:], in_=grouped[:])
+            return codes, scales
+
+        def section(s):
+            return slice(s * P, (s + 1) * P)
+
+        proj = product_banks.tile([P, ROW_GROUPS, COLUMNS], F32)
+        for m in range(ROW_GROUPS):
+            h_codes, h_scales = quantise_transposed(h_tiles[m])
+            for g in range(FEATURE_PASSES):
+                nc.tensor.matmul_mx(
+                    out=proj[:, m, :],
+                    lhsT=h_codes[:, section(g)].bitcast(FP8X4),
+                    lhsT_scale=h_scales[:, section(g)],
+                    rhs=w_codes[:, section(g)].bitcast(FP8X4),
+                    rhs_scale=w_scales[:, section(g)],
+                    start=(g == 0),
+                    stop=(g == FEATURE_PASSES - 1),
+                )
+
+        adj_operands = [quantise_transposed(adj_rows) for adj_rows in adj_tiles]
+
+        proj_grouped = consts.tile([P, COLUMNS * PACK], BF16, align_bytes=64)
+        nc.vector.tensor_copy(
+            out=proj_grouped[:].rearrange("p (c m) -> p c m", m=PACK),
+            in_=proj[:].rearrange("p m c -> p c m"),
+        )
+        proj_codes = consts.tile([P, COLUMNS], U32, align_bytes=64)
+        proj_scales = consts.tile([P, COLUMNS], U8, align_bytes=64)
+        nc.vector.quantize_mx(
+            out=proj_codes[:].bitcast(FP8X4), scales=proj_scales[:], in_=proj_grouped[:]
+        )
+
+        result_sums = product_banks.tile([P, ROW_GROUPS, COLUMNS], F32)
+        result = consts.tile([P, ROW_GROUPS, COLUMNS], F32)
+        for a, (adj_codes, adj_scales) in enumerate(adj_operands):
+            for s in range(SECTIONS):
+                nc.tensor.matmul_mx(
+                    out=result_sums[:, a * SECTIONS + s, :],
+                    lhsT=adj_codes[:, section(s)].bitcast(FP8X4),
+                    lhsT_scale=adj_scales[:, section(s)],
+                    rhs=proj_codes[:].bitcast(FP8X4),
+                    rhs_scale=proj_scales[:],
+                    start=True,
+                    stop=True,
+                )
+        for a in range(ROW_GROUPS // SECTIONS):
+            groups = slice(a * SECTIONS, (a + 1) * SECTIONS)
+            nc.vector.tensor_tensor(
+                out=result[:, groups, :],
+                in0=result_sums[:, groups, :],
+                in1=bias[:].unsqueeze(1).to_broadcast([P, SECTIONS, COLUMNS]),
+                op=mybir.AluOpType.add,
+            )
+            nc.sync.dma_start(
+                out=out.rearrange("(p m) c -> p m c", m=ROW_GROUPS)[:, groups, :],
+                in_=result[:, groups, :],
+            )

@@ -31,7 +31,7 @@ def tile_graphlayer_s_kernel(tc, H, adj, W, b, out):
         loads = ctx.enter_context(tc.tile_pool(name="loads", bufs=6))
         stage = ctx.enter_context(tc.tile_pool(name="stage", bufs=6))
         operands = ctx.enter_context(tc.tile_pool(name="operands", bufs=6))
-        flipped_banks = ctx.enter_context(tc.psum_pool(name="flipped", bufs=6))
+        flipped_banks = ctx.enter_context(tc.psum_pool(name="flipped", bufs=5))
         product_banks = ctx.enter_context(tc.psum_pool(name="products", bufs=1))
 
         w_raw = consts.tile([P, HEADS * FEATURE_PASSES, PACK * HEAD_WIDTH], BF16)
@@ -52,11 +52,19 @@ def tile_graphlayer_s_kernel(tc, H, adj, W, b, out):
                 in_=adj.rearrange("(p a s) n -> a p (s n)", a=ROW_GROUPS // SECTIONS, s=SECTIONS)[a],
             )
             adj_tiles.append(adj_rows)
-        bias = consts.tile([P, COLUMNS], BF16)
-        nc.scalar.dma_start(out=bias[:], in_=b.rearrange("h d -> (h d)").partition_broadcast(P))
+        bias_row = consts.tile([P, COLUMNS], BF16)
+        nc.vector.memset(bias_row[:], 0.0)
+        nc.scalar.dma_start(out=bias_row[0:1, :], in_=b.rearrange("h d -> (h d)").unsqueeze(0))
 
         identity = consts.tile([P, P], F32)
         make_identity(nc, identity[:])
+
+        ones = consts.tile([P, P], BF16)
+        nc.vector.memset(ones[:], 1.0)
+        bias_sums = product_banks.tile([P, COLUMNS], F32)
+        nc.tensor.matmul(out=bias_sums[:], lhsT=ones[:], rhs=bias_row[:], start=True, stop=True)
+        bias = consts.tile([P, COLUMNS], F32)
+        nc.vector.tensor_copy(out=bias[:], in_=bias_sums[:])
 
         w_grouped = consts.tile([P, FEATURE_PASSES * COLUMNS * PACK], BF16, align_bytes=64)
         for g in range(FEATURE_PASSES):

@@ -33,6 +33,7 @@ def tile_graphlayer_s_kernel(tc, H, adj, W, b, out):
         operands = ctx.enter_context(tc.tile_pool(name="operands", bufs=6))
         flipped_banks = ctx.enter_context(tc.psum_pool(name="flipped", bufs=5))
         product_banks = ctx.enter_context(tc.psum_pool(name="products", bufs=1))
+        ctx.enter_context(tc.manual_schedule())
 
         w_raw = consts.tile([P, HEADS * FEATURE_PASSES, PACK * HEAD_WIDTH], BF16)
         nc.sync.dma_start(
@@ -58,13 +59,8 @@ def tile_graphlayer_s_kernel(tc, H, adj, W, b, out):
 
         identity = consts.tile([P, P], F32)
         make_identity(nc, identity[:])
-
         ones = consts.tile([P, P], BF16)
         nc.vector.memset(ones[:], 1.0)
-        bias_sums = product_banks.tile([P, COLUMNS], F32)
-        nc.tensor.matmul(out=bias_sums[:], lhsT=ones[:], rhs=bias_row[:], start=True, stop=True)
-        bias = consts.tile([P, COLUMNS], F32)
-        nc.vector.tensor_copy(out=bias[:], in_=bias_sums[:])
 
         w_grouped = consts.tile([P, FEATURE_PASSES * COLUMNS * PACK], BF16, align_bytes=64)
         for g in range(FEATURE_PASSES):
@@ -99,9 +95,16 @@ def tile_graphlayer_s_kernel(tc, H, adj, W, b, out):
         def section(s):
             return slice(s * P, (s + 1) * P)
 
+        h_operands = [quantise_transposed(h_rows) for h_rows in h_tiles]
+        adj_operands = [quantise_transposed(adj_rows) for adj_rows in adj_tiles]
+
+        bias_sums = product_banks.tile([P, COLUMNS], F32)
+        nc.tensor.matmul(out=bias_sums[:], lhsT=ones[:], rhs=bias_row[:], start=True, stop=True)
+        bias = consts.tile([P, COLUMNS], F32)
+        nc.vector.tensor_copy(out=bias[:], in_=bias_sums[:])
+
         proj = product_banks.tile([P, ROW_GROUPS, COLUMNS], F32)
-        for m in range(ROW_GROUPS):
-            h_codes, h_scales = quantise_transposed(h_tiles[m])
+        for m, (h_codes, h_scales) in enumerate(h_operands):
             for g in range(FEATURE_PASSES):
                 nc.tensor.matmul_mx(
                     out=proj[:, m, :],
@@ -112,8 +115,6 @@ def tile_graphlayer_s_kernel(tc, H, adj, W, b, out):
                     start=(g == 0),
                     stop=(g == FEATURE_PASSES - 1),
                 )
-
-        adj_operands = [quantise_transposed(adj_rows) for adj_rows in adj_tiles]
 
         proj_grouped = consts.tile([P, COLUMNS * PACK], BF16, align_bytes=64)
         nc.vector.tensor_copy(

@@ -36,7 +36,7 @@ def tile_graphlayer_s_kernel(tc, H, adj, W, b, out):
         ctx.enter_context(tc.manual_schedule())
 
         w_raw = consts.tile([P, HEADS * FEATURE_PASSES, PACK * HEAD_WIDTH], BF16)
-        nc.sync.dma_start(
+        nc.scalar.dma_start(
             out=w_raw[:],
             in_=W.rearrange("h (g p j) d -> p (h g) (j d)", g=FEATURE_PASSES, j=PACK),
         )

@@ -31,8 +31,9 @@ def tile_graphlayer_s_kernel(tc, H, adj, W, b, out):
         loads = ctx.enter_context(tc.tile_pool(name="loads", bufs=6))
         stage = ctx.enter_context(tc.tile_pool(name="stage", bufs=6))
         operands = ctx.enter_context(tc.tile_pool(name="operands", bufs=6))
-        flipped_banks = ctx.enter_context(tc.psum_pool(name="flipped", bufs=5))
+        flipped_banks = ctx.enter_context(tc.psum_pool(name="flipped", bufs=4))
         product_banks = ctx.enter_context(tc.psum_pool(name="products", bufs=1))
+        result_banks = ctx.enter_context(tc.psum_pool(name="results", bufs=2))
         ctx.enter_context(tc.manual_schedule())
 
         w_raw = consts.tile([P, HEADS * FEATURE_PASSES, PACK * HEAD_WIDTH], BF16)
@@ -76,7 +77,7 @@ def tile_graphlayer_s_kernel(tc, H, adj, W, b, out):
         w_scales = consts.tile([P, FEATURE_PASSES * COLUMNS], U8, align_bytes=64)
         nc.vector.quantize_mx(out=w_codes[:].bitcast(FP8X4), scales=w_scales[:], in_=w_grouped[:])
 
-        def quantise_transposed(rows):
+        def transpose_rows(rows):
             words = rows[:].bitcast(F32).rearrange("r (s p u) -> r s p u", s=SECTIONS, u=WORDS)
             flipped = flipped_banks.tile([P, SECTIONS, WORDS, P], F32)
             for s in range(SECTIONS):
@@ -87,6 +88,9 @@ def tile_graphlayer_s_kernel(tc, H, adj, W, b, out):
                 out=grouped[:].bitcast(F32).rearrange("p (s r u) -> p s r u", s=SECTIONS, u=WORDS),
                 in_=flipped[:].rearrange("p s u r -> p s r u"),
             )
+            return grouped
+
+        def quantise(grouped):
             codes = operands.tile([P, SECTIONS * P], U32, align_bytes=64)
             scales = operands.tile([P, SECTIONS * P], U8, align_bytes=64)
             nc.vector.quantize_mx(out=codes[:].bitcast(FP8X4), scales=scales[:], in_=grouped[:])
@@ -95,8 +99,9 @@ def tile_graphlayer_s_kernel(tc, H, adj, W, b, out):
         def section(s):
             return slice(s * P, (s + 1) * P)
 
-        h_operands = [quantise_transposed(h_rows) for h_rows in h_tiles]
-        adj_operands = [quantise_transposed(adj_rows) for adj_rows in adj_tiles]
+        h_operands = [quantise(transpose_rows(h_rows)) for h_rows in h_tiles]
+        adj_grouped = [transpose_rows(adj_rows) for adj_rows in adj_tiles]
+        adj_operands = [quantise(adj_grouped[0])]
 
         bias_sums = product_banks.tile([P, COLUMNS], F32)
         nc.tensor.matmul(out=bias_sums[:], lhsT=ones[:], rhs=bias_row[:], start=True, stop=True)
@@ -121,18 +126,19 @@ def tile_graphlayer_s_kernel(tc, H, adj, W, b, out):
             out=proj_grouped[:].rearrange("p (c m) -> p c m", m=PACK),
             in_=proj[:].rearrange("p m c -> p c m"),
         )
+        adj_operands.append(quantise(adj_grouped[1]))
         proj_codes = consts.tile([P, COLUMNS], U32, align_bytes=64)
         proj_scales = consts.tile([P, COLUMNS], U8, align_bytes=64)
         nc.vector.quantize_mx(
             out=proj_codes[:].bitcast(FP8X4), scales=proj_scales[:], in_=proj_grouped[:]
         )
 
-        result_sums = product_banks.tile([P, ROW_GROUPS, COLUMNS], F32)
         result = consts.tile([P, ROW_GROUPS, COLUMNS], F32)
         for a, (adj_codes, adj_scales) in enumerate(adj_operands):
+            result_sums = result_banks.tile([P, SECTIONS, COLUMNS], F32)
             for s in range(SECTIONS):
                 nc.tensor.matmul_mx(
-                    out=result_sums[:, a * SECTIONS + s, :],
+                    out=result_sums[:, s, :],
                     lhsT=adj_codes[:, section(s)].bitcast(FP8X4),
                     lhsT_scale=adj_scales[:, section(s)],
                     rhs=proj_codes[:].bitcast(FP8X4),
@@ -140,11 +146,10 @@ def tile_graphlayer_s_kernel(tc, H, adj, W, b, out):
                     start=True,
                     stop=True,
                 )
-        for a in range(ROW_GROUPS // SECTIONS):
             groups = slice(a * SECTIONS, (a + 1) * SECTIONS)
             nc.vector.tensor_tensor(
                 out=result[:, groups, :],
-                in0=result_sums[:, groups, :],
+                in0=result_sums[:],
                 in1=bias[:].unsqueeze(1).to_broadcast([P, SECTIONS, COLUMNS]),
                 op=mybir.AluOpType.add,
             )

@@ -100,13 +100,11 @@ def tile_graphlayer_s_kernel(tc, H, adj, W, b, out):
             return slice(s * P, (s + 1) * P)
 
         h_operands = [quantise(transpose_rows(h_rows)) for h_rows in h_tiles]
-        adj_grouped = [transpose_rows(adj_rows) for adj_rows in adj_tiles]
-        adj_operands = [quantise(adj_grouped[0])]
+        adj_operands = [quantise(transpose_rows(adj_tiles[0]))]
 
         bias_sums = product_banks.tile([P, COLUMNS], F32)
         nc.tensor.matmul(out=bias_sums[:], lhsT=ones[:], rhs=bias_row[:], start=True, stop=True)
         bias = consts.tile([P, COLUMNS], F32)
-        nc.vector.tensor_copy(out=bias[:], in_=bias_sums[:])
 
         proj = product_banks.tile([P, ROW_GROUPS, COLUMNS], F32)
         for m, (h_codes, h_scales) in enumerate(h_operands):
@@ -126,12 +124,13 @@ def tile_graphlayer_s_kernel(tc, H, adj, W, b, out):
             out=proj_grouped[:].rearrange("p (c m) -> p c m", m=PACK),
             in_=proj[:].rearrange("p m c -> p c m"),
         )
-        adj_operands.append(quantise(adj_grouped[1]))
+        nc.vector.tensor_copy(out=bias[:], in_=bias_sums[:])
         proj_codes = consts.tile([P, COLUMNS], U32, align_bytes=64)
         proj_scales = consts.tile([P, COLUMNS], U8, align_bytes=64)
         nc.vector.quantize_mx(
             out=proj_codes[:].bitcast(FP8X4), scales=proj_scales[:], in_=proj_grouped[:]
         )
+        adj_operands.append(quantise(transpose_rows(adj_tiles[1])))
 
         result = consts.tile([P, ROW_GROUPS, COLUMNS], F32)
         for a, (adj_codes, adj_scales) in enumerate(adj_operands):

@@ -19,7 +19,6 @@ NODES, FEATURES, HEADS, HEAD_WIDTH = 512, 1024, 8, 16
 COLUMNS = HEADS * HEAD_WIDTH
 ROW_GROUPS = NODES // P
 FEATURE_PASSES = FEATURES // K_PASS
-SECTIONS = 2
 
 FLOPS = 2 * NODES * FEATURES * COLUMNS + 2 * NODES * NODES * COLUMNS
 
@@ -28,12 +27,11 @@ def tile_graphlayer_s_kernel(tc, H, adj, W, b, out):
     nc = tc.nc
     with ExitStack() as ctx:
         consts = ctx.enter_context(tc.tile_pool(name="consts", bufs=1))
-        loads = ctx.enter_context(tc.tile_pool(name="loads", bufs=6))
-        stage = ctx.enter_context(tc.tile_pool(name="stage", bufs=6))
-        operands = ctx.enter_context(tc.tile_pool(name="operands", bufs=6))
-        flipped_banks = ctx.enter_context(tc.psum_pool(name="flipped", bufs=4))
+        loads = ctx.enter_context(tc.tile_pool(name="loads", bufs=7))
+        stage = ctx.enter_context(tc.tile_pool(name="stage", bufs=7))
+        operands = ctx.enter_context(tc.tile_pool(name="operands", bufs=7))
+        banks = ctx.enter_context(tc.psum_pool(name="banks", bufs=5))
         product_banks = ctx.enter_context(tc.psum_pool(name="products", bufs=1))
-        result_banks = ctx.enter_context(tc.psum_pool(name="results", bufs=2))
         ctx.enter_context(tc.manual_schedule())
 
         w_raw = consts.tile([P, HEADS * FEATURE_PASSES, PACK * HEAD_WIDTH], BF16)
@@ -43,21 +41,19 @@ def tile_graphlayer_s_kernel(tc, H, adj, W, b, out):
         )
         h_tiles = []
         for m in range(ROW_GROUPS):
-            h_rows = loads.tile([P, SECTIONS * K_PASS], BF16, tag="rows")
+            h_rows = loads.tile([P, 2 * K_PASS], BF16, tag="rows")
             nc.sync.dma_start(out=h_rows[:], in_=H.rearrange("(p m) k -> m p k", m=ROW_GROUPS)[m])
             h_tiles.append(h_rows)
-        adj_tiles = []
-        for a in range(ROW_GROUPS // SECTIONS):
-            adj_rows = loads.tile([P, SECTIONS * K_PASS], BF16, tag="rows")
-            nc.sync.dma_start(
-                out=adj_rows[:],
-                in_=adj.rearrange("(p a s) n -> a p (s n)", a=ROW_GROUPS // SECTIONS, s=SECTIONS)[a],
-            )
-            adj_tiles.append(adj_rows)
+        adj_01 = loads.tile([P, 2 * K_PASS], BF16, tag="rows")
+        nc.sync.dma_start(out=adj_01[:], in_=adj.rearrange("(p a s) n -> a p (s n)", a=2, s=2)[0])
+        adj_2 = loads.tile([P, K_PASS], BF16, tag="rows")
+        nc.sync.dma_start(out=adj_2[:], in_=adj.rearrange("(p m) n -> m p n", m=ROW_GROUPS)[2])
+        adj_3 = loads.tile([P, K_PASS], BF16, tag="rows")
+        nc.sync.dma_start(out=adj_3[:], in_=adj.rearrange("(p m) n -> m p n", m=ROW_GROUPS)[3])
+
         bias_row = consts.tile([P, COLUMNS], BF16)
         nc.vector.memset(bias_row[:], 0.0)
         nc.scalar.dma_start(out=bias_row[0:1, :], in_=b.rearrange("h d -> (h d)").unsqueeze(0))
-
         identity = consts.tile([P, P], F32)
         make_identity(nc, identity[:])
         ones = consts.tile([P, P], BF16)
@@ -69,73 +65,75 @@ def tile_graphlayer_s_kernel(tc, H, adj, W, b, out):
                 out=w_grouped[:].rearrange(
                     "p (g h d j) -> p g h d j", g=FEATURE_PASSES, h=HEADS, j=PACK
                 )[:, g],
-                in_=w_raw[:].rearrange(
-                    "p (h g) (j d) -> p g h d j", g=FEATURE_PASSES, j=PACK
-                )[:, g],
+                in_=w_raw[:].rearrange("p (h g) (j d) -> p g h d j", g=FEATURE_PASSES, j=PACK)[:, g],
             )
         w_codes = consts.tile([P, FEATURE_PASSES * COLUMNS], U32, align_bytes=64)
         w_scales = consts.tile([P, FEATURE_PASSES * COLUMNS], U8, align_bytes=64)
         nc.vector.quantize_mx(out=w_codes[:].bitcast(FP8X4), scales=w_scales[:], in_=w_grouped[:])
 
-        def transpose_rows(rows):
-            words = rows[:].bitcast(F32).rearrange("r (s p u) -> r s p u", s=SECTIONS, u=WORDS)
-            flipped = flipped_banks.tile([P, SECTIONS, WORDS, P], F32)
-            for s in range(SECTIONS):
+        def flip_and_empty(rows, sections):
+            words = rows[:].bitcast(F32).rearrange("r (s p u) -> r s p u", s=sections, u=WORDS)
+            flipped = banks.tile([P, sections, WORDS, P], F32, tag="bank")
+            for s in range(sections):
                 for u in range(WORDS):
                     nc.tensor.transpose(flipped[:, s, u, :], words[:, s, :, u], identity[:])
-            grouped = stage.tile([P, SECTIONS * P * PACK], BF16, align_bytes=64)
+            grouped = stage.tile([P, sections * P * PACK], BF16, align_bytes=64, tag="grouped")
             nc.scalar.copy(
-                out=grouped[:].bitcast(F32).rearrange("p (s r u) -> p s r u", s=SECTIONS, u=WORDS),
+                out=grouped[:].bitcast(F32).rearrange("p (s r u) -> p s r u", s=sections, u=WORDS),
                 in_=flipped[:].rearrange("p s u r -> p s r u"),
             )
             return grouped
 
-        def quantise(grouped):
-            codes = operands.tile([P, SECTIONS * P], U32, align_bytes=64)
-            scales = operands.tile([P, SECTIONS * P], U8, align_bytes=64)
+        def quantise(grouped, sections):
+            codes = operands.tile([P, sections * P], U32, align_bytes=64, tag="codes")
+            scales = operands.tile([P, sections * P], U8, align_bytes=64, tag="scales")
             nc.vector.quantize_mx(out=codes[:].bitcast(FP8X4), scales=scales[:], in_=grouped[:])
             return codes, scales
 
         def section(s):
             return slice(s * P, (s + 1) * P)
 
-        h_operands = [quantise(transpose_rows(h_rows)) for h_rows in h_tiles]
-        adj_operands = [quantise(transpose_rows(adj_tiles[0]))]
+        h_operands = [quantise(flip_and_empty(h_rows, 2), 2) for h_rows in h_tiles]
+        adj_operands = [quantise(flip_and_empty(adj_01, 2), 2)]
 
         bias_sums = product_banks.tile([P, COLUMNS], F32)
         nc.tensor.matmul(out=bias_sums[:], lhsT=ones[:], rhs=bias_row[:], start=True, stop=True)
         bias = consts.tile([P, COLUMNS], F32)
 
-        proj = product_banks.tile([P, ROW_GROUPS, COLUMNS], F32)
-        for m, (h_codes, h_scales) in enumerate(h_operands):
-            for g in range(FEATURE_PASSES):
-                nc.tensor.matmul_mx(
-                    out=proj[:, m, :],
-                    lhsT=h_codes[:, section(g)].bitcast(FP8X4),
-                    lhsT_scale=h_scales[:, section(g)],
-                    rhs=w_codes[:, section(g)].bitcast(FP8X4),
-                    rhs_scale=w_scales[:, section(g)],
-                    start=(g == 0),
-                    stop=(g == FEATURE_PASSES - 1),
-                )
-
         proj_grouped = consts.tile([P, COLUMNS * PACK], BF16, align_bytes=64)
-        nc.vector.tensor_copy(
-            out=proj_grouped[:].rearrange("p (c m) -> p c m", m=PACK),
-            in_=proj[:].rearrange("p m c -> p c m"),
-        )
+        proj_to = proj_grouped[:].rearrange("p (c a i) -> p a c i", a=2, i=2)
+        proj_low = product_banks.tile([P, 2, COLUMNS], F32)
+        proj_high = product_banks.tile([P, 2, COLUMNS], F32)
+        for a, (proj_half, copy) in enumerate(
+            ((proj_low, nc.scalar.copy), (proj_high, nc.vector.tensor_copy))
+        ):
+            for i in range(2):
+                h_codes, h_scales = h_operands[2 * a + i]
+                for g in range(FEATURE_PASSES):
+                    nc.tensor.matmul_mx(
+                        out=proj_half[:, i, :],
+                        lhsT=h_codes[:, section(g)].bitcast(FP8X4),
+                        lhsT_scale=h_scales[:, section(g)],
+                        rhs=w_codes[:, section(g)].bitcast(FP8X4),
+                        rhs_scale=w_scales[:, section(g)],
+                        start=(g == 0),
+                        stop=(g == FEATURE_PASSES - 1),
+                    )
+            copy(out=proj_to[:, a], in_=proj_half[:].rearrange("p i c -> p c i"))
         nc.vector.tensor_copy(out=bias[:], in_=bias_sums[:])
         proj_codes = consts.tile([P, COLUMNS], U32, align_bytes=64)
         proj_scales = consts.tile([P, COLUMNS], U8, align_bytes=64)
         nc.vector.quantize_mx(
             out=proj_codes[:].bitcast(FP8X4), scales=proj_scales[:], in_=proj_grouped[:]
         )
-        adj_operands.append(quantise(transpose_rows(adj_tiles[1])))
+        adj_operands.append(quantise(flip_and_empty(adj_2, 1), 1))
+        adj_operands.append(quantise(flip_and_empty(adj_3, 1), 1))
 
         result = consts.tile([P, ROW_GROUPS, COLUMNS], F32)
-        for a, (adj_codes, adj_scales) in enumerate(adj_operands):
-            result_sums = result_banks.tile([P, SECTIONS, COLUMNS], F32)
-            for s in range(SECTIONS):
+        first_group = 0
+        for (adj_codes, adj_scales), sections in zip(adj_operands, (2, 1, 1)):
+            result_sums = banks.tile([P, sections, COLUMNS], F32, tag="bank")
+            for s in range(sections):
                 nc.tensor.matmul_mx(
                     out=result_sums[:, s, :],
                     lhsT=adj_codes[:, section(s)].bitcast(FP8X4),
@@ -145,11 +143,12 @@ def tile_graphlayer_s_kernel(tc, H, adj, W, b, out):
                     start=True,
                     stop=True,
                 )
-            groups = slice(a * SECTIONS, (a + 1) * SECTIONS)
+            groups = slice(first_group, first_group + sections)
+            first_group += sections
             nc.vector.tensor_tensor(
                 out=result[:, groups, :],
                 in0=result_sums[:],
-                in1=bias[:].unsqueeze(1).to_broadcast([P, SECTIONS, COLUMNS]),
+                in1=bias[:].unsqueeze(1).to_broadcast([P, sections, COLUMNS]),
                 op=mybir.AluOpType.add,
             )
             nc.sync.dma_start(

@@ -27,9 +27,9 @@ def tile_graphlayer_s_kernel(tc, H, adj, W, b, out):
     nc = tc.nc
     with ExitStack() as ctx:
         consts = ctx.enter_context(tc.tile_pool(name="consts", bufs=1))
-        loads = ctx.enter_context(tc.tile_pool(name="loads", bufs=7))
-        stage = ctx.enter_context(tc.tile_pool(name="stage", bufs=7))
-        operands = ctx.enter_context(tc.tile_pool(name="operands", bufs=7))
+        loads = ctx.enter_context(tc.tile_pool(name="loads", bufs=8))
+        stage = ctx.enter_context(tc.tile_pool(name="stage", bufs=8))
+        operands = ctx.enter_context(tc.tile_pool(name="operands", bufs=8))
         banks = ctx.enter_context(tc.psum_pool(name="banks", bufs=5))
         product_banks = ctx.enter_context(tc.psum_pool(name="products", bufs=1))
         ctx.enter_context(tc.manual_schedule())
@@ -40,10 +40,20 @@ def tile_graphlayer_s_kernel(tc, H, adj, W, b, out):
             in_=W.rearrange("h (g p j) d -> p (h g) (j d)", g=FEATURE_PASSES, j=PACK),
         )
         h_tiles = []
-        for m in range(ROW_GROUPS):
+        for m in range(ROW_GROUPS - 1):
             h_rows = loads.tile([P, 2 * K_PASS], BF16, tag="rows")
             nc.sync.dma_start(out=h_rows[:], in_=H.rearrange("(p m) k -> m p k", m=ROW_GROUPS)[m])
             h_tiles.append(h_rows)
+        h_last = []
+        for g in range(FEATURE_PASSES):
+            h_rows = loads.tile([P, K_PASS], BF16, tag="rows")
+            nc.sync.dma_start(
+                out=h_rows[:],
+                in_=H.rearrange("(p m) (g k) -> m g p k", m=ROW_GROUPS, g=FEATURE_PASSES)[
+                    ROW_GROUPS - 1, g
+                ],
+            )
+            h_last.append(h_rows)
         adj_01 = loads.tile([P, 2 * K_PASS], BF16, tag="rows")
         nc.sync.dma_start(out=adj_01[:], in_=adj.rearrange("(p a s) n -> a p (s n)", a=2, s=2)[0])
         adj_2 = loads.tile([P, K_PASS], BF16, tag="rows")
@@ -93,7 +103,11 @@ def tile_graphlayer_s_kernel(tc, H, adj, W, b, out):
         def section(s):
             return slice(s * P, (s + 1) * P)
 
-        h_operands = [quantise(flip_and_empty(h_rows, 2), 2) for h_rows in h_tiles]
+        h_passes = []
+        for h_rows in h_tiles:
+            h_codes, h_scales = quantise(flip_and_empty(h_rows, 2), 2)
+            h_passes.append([(h_codes, h_scales, section(g)) for g in range(FEATURE_PASSES)])
+        h_passes.append([quantise(flip_and_empty(h_rows, 1), 1) + (section(0),) for h_rows in h_last])
         adj_operands = [quantise(flip_and_empty(adj_01, 2), 2)]
 
         bias_sums = product_banks.tile([P, COLUMNS], F32)
@@ -105,15 +119,15 @@ def tile_graphlayer_s_kernel(tc, H, adj, W, b, out):
         proj_low = product_banks.tile([P, 2, COLUMNS], F32)
         proj_high = product_banks.tile([P, 2, COLUMNS], F32)
         for a, (proj_half, copy) in enumerate(
-            ((proj_low, nc.scalar.copy), (proj_high, nc.vector.tensor_copy))
+            ((proj_low, nc.vector.tensor_copy), (proj_high, nc.scalar.copy))
         ):
             for i in range(2):
-                h_codes, h_scales = h_operands[2 * a + i]
                 for g in range(FEATURE_PASSES):
+                    h_codes, h_scales, columns = h_passes[2 * a + i][g]
                     nc.tensor.matmul_mx(
                         out=proj_half[:, i, :],
-                        lhsT=h_codes[:, section(g)].bitcast(FP8X4),
-                        lhsT_scale=h_scales[:, section(g)],
+                        lhsT=h_codes[:, columns].bitcast(FP8X4),
+                        lhsT_scale=h_scales[:, columns],
                         rhs=w_codes[:, section(g)].bitcast(FP8X4),
                         rhs_scale=w_scales[:, section(g)],
                         start=(g == 0),

@@ -69,18 +69,6 @@ def tile_graphlayer_s_kernel(tc, H, adj, W, b, out):
         ones = consts.tile([P, P], BF16)
         nc.vector.memset(ones[:], 1.0)
 
-        w_grouped = consts.tile([P, FEATURE_PASSES * COLUMNS * PACK], BF16, align_bytes=64)
-        for g in range(FEATURE_PASSES):
-            nc.vector.tensor_copy(
-                out=w_grouped[:].rearrange(
-                    "p (g h d j) -> p g h d j", g=FEATURE_PASSES, h=HEADS, j=PACK
-                )[:, g],
-                in_=w_raw[:].rearrange("p (h g) (j d) -> p g h d j", g=FEATURE_PASSES, j=PACK)[:, g],
-            )
-        w_codes = consts.tile([P, FEATURE_PASSES * COLUMNS], U32, align_bytes=64)
-        w_scales = consts.tile([P, FEATURE_PASSES * COLUMNS], U8, align_bytes=64)
-        nc.vector.quantize_mx(out=w_codes[:].bitcast(FP8X4), scales=w_scales[:], in_=w_grouped[:])
-
         def flip_and_empty(rows, sections):
             words = rows[:].bitcast(F32).rearrange("r (s p u) -> r s p u", s=sections, u=WORDS)
             flipped = banks.tile([P, sections, WORDS, P], F32, tag="bank")
@@ -100,13 +88,29 @@ def tile_graphlayer_s_kernel(tc, H, adj, W, b, out):
             nc.vector.quantize_mx(out=codes[:].bitcast(FP8X4), scales=scales[:], in_=grouped[:])
             return codes, scales
 
+        def quantise_w():
+            w_grouped = consts.tile([P, FEATURE_PASSES * COLUMNS * PACK], BF16, align_bytes=64)
+            for g in range(FEATURE_PASSES):
+                nc.vector.tensor_copy(
+                    out=w_grouped[:].rearrange(
+                        "p (g h d j) -> p g h d j", g=FEATURE_PASSES, h=HEADS, j=PACK
+                    )[:, g],
+                    in_=w_raw[:].rearrange("p (h g) (j d) -> p g h d j", g=FEATURE_PASSES, j=PACK)[:, g],
+                )
+            w_codes = consts.tile([P, FEATURE_PASSES * COLUMNS], U32, align_bytes=64)
+            w_scales = consts.tile([P, FEATURE_PASSES * COLUMNS], U8, align_bytes=64)
+            nc.vector.quantize_mx(out=w_codes[:].bitcast(FP8X4), scales=w_scales[:], in_=w_grouped[:])
+            return w_codes, w_scales
+
         def section(s):
             return slice(s * P, (s + 1) * P)
 
         h_passes = []
-        for h_rows in h_tiles:
+        for m, h_rows in enumerate(h_tiles):
             h_codes, h_scales = quantise(flip_and_empty(h_rows, 2), 2)
             h_passes.append([(h_codes, h_scales, section(g)) for g in range(FEATURE_PASSES)])
+            if m == 0:
+                w_codes, w_scales = quantise_w()
         h_passes.append([quantise(flip_and_empty(h_rows, 1), 1) + (section(0),) for h_rows in h_last])
         adj_operands = [quantise(flip_and_empty(adj_01, 2), 2)]
 

@@ -35,15 +35,16 @@ def tile_graphlayer_s_kernel(tc, H, adj, W, b, out):
         ctx.enter_context(tc.manual_schedule())
 
         w_raw = consts.tile([P, HEADS * FEATURE_PASSES, PACK * HEAD_WIDTH], BF16)
-        nc.scalar.dma_start(
-            out=w_raw[:],
-            in_=W.rearrange("h (g p j) d -> p (h g) (j d)", g=FEATURE_PASSES, j=PACK),
-        )
         h_tiles = []
         for m in range(ROW_GROUPS - 1):
             h_rows = loads.tile([P, 2 * K_PASS], BF16, tag="rows")
             nc.sync.dma_start(out=h_rows[:], in_=H.rearrange("(p m) k -> m p k", m=ROW_GROUPS)[m])
             h_tiles.append(h_rows)
+            if m == 1:
+                nc.sync.dma_start(
+                    out=w_raw[:],
+                    in_=W.rearrange("h (g p j) d -> p (h g) (j d)", g=FEATURE_PASSES, j=PACK),
+                )
         h_last = []
         for g in range(FEATURE_PASSES):
             h_rows = loads.tile([P, K_PASS], BF16, tag="rows")
@@ -109,7 +110,7 @@ def tile_graphlayer_s_kernel(tc, H, adj, W, b, out):
         for m, h_rows in enumerate(h_tiles):
             h_codes, h_scales = quantise(flip_and_empty(h_rows, 2), 2)
             h_passes.append([(h_codes, h_scales, section(g)) for g in range(FEATURE_PASSES)])
-            if m == 0:
+            if m == 1:
                 w_codes, w_scales = quantise_w()
         h_passes.append([quantise(flip_and_empty(h_rows, 1), 1) + (section(0),) for h_rows in h_last])
         adj_operands = [quantise(flip_and_empty(adj_01, 2), 2)]

@@ -40,7 +40,7 @@ def tile_graphlayer_s_kernel(tc, H, adj, W, b, out):
             h_rows = loads.tile([P, 2 * K_PASS], BF16, tag="rows")
             nc.sync.dma_start(out=h_rows[:], in_=H.rearrange("(p m) k -> m p k", m=ROW_GROUPS)[m])
             h_tiles.append(h_rows)
-            if m == 1:
+            if m == 2:
                 nc.sync.dma_start(
                     out=w_raw[:],
                     in_=W.rearrange("h (g p j) d -> p (h g) (j d)", g=FEATURE_PASSES, j=PACK),
@@ -57,10 +57,8 @@ def tile_graphlayer_s_kernel(tc, H, adj, W, b, out):
             h_last.append(h_rows)
         adj_01 = loads.tile([P, 2 * K_PASS], BF16, tag="rows")
         nc.sync.dma_start(out=adj_01[:], in_=adj.rearrange("(p a s) n -> a p (s n)", a=2, s=2)[0])
-        adj_2 = loads.tile([P, K_PASS], BF16, tag="rows")
-        nc.sync.dma_start(out=adj_2[:], in_=adj.rearrange("(p m) n -> m p n", m=ROW_GROUPS)[2])
-        adj_3 = loads.tile([P, K_PASS], BF16, tag="rows")
-        nc.sync.dma_start(out=adj_3[:], in_=adj.rearrange("(p m) n -> m p n", m=ROW_GROUPS)[3])
+        adj_23 = loads.tile([P, 2 * K_PASS], BF16, tag="rows")
+        nc.sync.dma_start(out=adj_23[:], in_=adj.rearrange("(p a s) n -> a p (s n)", a=2, s=2)[1])
 
         bias_row = consts.tile([P, COLUMNS], BF16)
         nc.vector.memset(bias_row[:], 0.0)
@@ -71,7 +69,7 @@ def tile_graphlayer_s_kernel(tc, H, adj, W, b, out):
         nc.vector.memset(ones[:], 1.0)
 
         def flip_and_empty(rows, sections):
-            words = rows[:].bitcast(F32).rearrange("r (s p u) -> r s p u", s=sections, u=WORDS)
+            words = rows.bitcast(F32).rearrange("r (s p u) -> r s p u", s=sections, u=WORDS)
             flipped = banks.tile([P, sections, WORDS, P], F32, tag="bank")
             for s in range(sections):
                 for u in range(WORDS):
@@ -108,12 +106,13 @@ def tile_graphlayer_s_kernel(tc, H, adj, W, b, out):
 
         h_passes = []
         for m, h_rows in enumerate(h_tiles):
-            h_codes, h_scales = quantise(flip_and_empty(h_rows, 2), 2)
+            h_codes, h_scales = quantise(flip_and_empty(h_rows[:], 2), 2)
             h_passes.append([(h_codes, h_scales, section(g)) for g in range(FEATURE_PASSES)])
             if m == 1:
                 w_codes, w_scales = quantise_w()
-        h_passes.append([quantise(flip_and_empty(h_rows, 1), 1) + (section(0),) for h_rows in h_last])
-        adj_operands = [quantise(flip_and_empty(adj_01, 2), 2)]
+        h_passes.append([quantise(flip_and_empty(h_rows[:], 1), 1) + (section(0),) for h_rows in h_last])
+        adj_01_grouped = flip_and_empty(adj_01[:], 2)
+        adj_operands = []
 
         bias_sums = product_banks.tile([P, COLUMNS], F32)
         nc.tensor.matmul(out=bias_sums[:], lhsT=ones[:], rhs=bias_row[:], start=True, stop=True)
@@ -139,14 +138,16 @@ def tile_graphlayer_s_kernel(tc, H, adj, W, b, out):
                         stop=(g == FEATURE_PASSES - 1),
                     )
             copy(out=proj_to[:, a], in_=proj_half[:].rearrange("p i c -> p c i"))
-        nc.vector.tensor_copy(out=bias[:], in_=bias_sums[:])
+            if a == 0:
+                adj_operands.append(quantise(adj_01_grouped, 2))
         proj_codes = consts.tile([P, COLUMNS], U32, align_bytes=64)
         proj_scales = consts.tile([P, COLUMNS], U8, align_bytes=64)
         nc.vector.quantize_mx(
             out=proj_codes[:].bitcast(FP8X4), scales=proj_scales[:], in_=proj_grouped[:]
         )
-        adj_operands.append(quantise(flip_and_empty(adj_2, 1), 1))
-        adj_operands.append(quantise(flip_and_empty(adj_3, 1), 1))
+        nc.vector.tensor_copy(out=bias[:], in_=bias_sums[:])
+        adj_operands.append(quantise(flip_and_empty(adj_23[:, 0:K_PASS], 1), 1))
+        adj_operands.append(quantise(flip_and_empty(adj_23[:, K_PASS : 2 * K_PASS], 1), 1))
 
         result = consts.tile([P, ROW_GROUPS, COLUMNS], F32)
         first_group = 0

@@ -36,7 +36,7 @@ def tile_graphlayer_s_kernel(tc, H, adj, W, b, out):
 
         w_raw = consts.tile([P, HEADS * FEATURE_PASSES, PACK * HEAD_WIDTH], BF16)
         h_tiles = []
-        for m in range(ROW_GROUPS - 1):
+        for m in range(ROW_GROUPS):
             h_rows = loads.tile([P, 2 * K_PASS], BF16, tag="rows")
             nc.sync.dma_start(out=h_rows[:], in_=H.rearrange("(p m) k -> m p k", m=ROW_GROUPS)[m])
             h_tiles.append(h_rows)
@@ -45,16 +45,6 @@ def tile_graphlayer_s_kernel(tc, H, adj, W, b, out):
                     out=w_raw[:],
                     in_=W.rearrange("h (g p j) d -> p (h g) (j d)", g=FEATURE_PASSES, j=PACK),
                 )
-        h_last = []
-        for g in range(FEATURE_PASSES):
-            h_rows = loads.tile([P, K_PASS], BF16, tag="rows")
-            nc.sync.dma_start(
-                out=h_rows[:],
-                in_=H.rearrange("(p m) (g k) -> m g p k", m=ROW_GROUPS, g=FEATURE_PASSES)[
-                    ROW_GROUPS - 1, g
-                ],
-            )
-            h_last.append(h_rows)
         adj_01 = loads.tile([P, 2 * K_PASS], BF16, tag="rows")
         nc.sync.dma_start(out=adj_01[:], in_=adj.rearrange("(p a s) n -> a p (s n)", a=2, s=2)[0])
         adj_23 = loads.tile([P, 2 * K_PASS], BF16, tag="rows")
@@ -105,18 +95,19 @@ def tile_graphlayer_s_kernel(tc, H, adj, W, b, out):
             return slice(s * P, (s + 1) * P)
 
         h_passes = []
-        for m, h_rows in enumerate(h_tiles):
+        for m, h_rows in enumerate(h_tiles[:-1]):
             h_codes, h_scales = quantise(flip_and_empty(h_rows[:], 2), 2)
             h_passes.append([(h_codes, h_scales, section(g)) for g in range(FEATURE_PASSES)])
             if m == 1:
                 w_codes, w_scales = quantise_w()
-        h_passes.append([quantise(flip_and_empty(h_rows[:], 1), 1) + (section(0),) for h_rows in h_last])
+        h_passes.append(
+            [
+                quantise(flip_and_empty(h_tiles[-1][:, g * K_PASS : (g + 1) * K_PASS], 1), 1) + (section(0),)
+                for g in range(FEATURE_PASSES)
+            ]
+        )
         adj_01_grouped = flip_and_empty(adj_01[:], 2)
         adj_operands = []
-
-        bias_sums = product_banks.tile([P, COLUMNS], F32)
-        nc.tensor.matmul(out=bias_sums[:], lhsT=ones[:], rhs=bias_row[:], start=True, stop=True)
-        bias = consts.tile([P, COLUMNS], F32)
 
         proj_grouped = consts.tile([P, COLUMNS * PACK], BF16, align_bytes=64)
         proj_to = proj_grouped[:].rearrange("p (c a i) -> p a c i", a=2, i=2)
@@ -145,9 +136,13 @@ def tile_graphlayer_s_kernel(tc, H, adj, W, b, out):
         nc.vector.quantize_mx(
             out=proj_codes[:].bitcast(FP8X4), scales=proj_scales[:], in_=proj_grouped[:]
         )
-        nc.vector.tensor_copy(out=bias[:], in_=bias_sums[:])
         adj_operands.append(quantise(flip_and_empty(adj_23[:, 0:K_PASS], 1), 1))
-        adj_operands.append(quantise(flip_and_empty(adj_23[:, K_PASS : 2 * K_PASS], 1), 1))
+        adj_3_grouped = flip_and_empty(adj_23[:, K_PASS : 2 * K_PASS], 1)
+        bias_sums = product_banks.tile([P, COLUMNS], F32)
+        nc.tensor.matmul(out=bias_sums[:], lhsT=ones[:], rhs=bias_row[:], start=True, stop=True)
+        bias = consts.tile([P, COLUMNS], F32)
+        nc.vector.tensor_copy(out=bias[:], in_=bias_sums[:])
+        adj_operands.append(quantise(adj_3_grouped, 1))
 
         result = consts.tile([P, ROW_GROUPS, COLUMNS], F32)
         first_group = 0

@@ -50,8 +50,30 @@ def tile_graphlayer_s_kernel(tc, H, adj, W, b, out):
         adj_23 = loads.tile([P, 2 * K_PASS], BF16, tag="rows")
         nc.sync.dma_start(out=adj_23[:], in_=adj.rearrange("(p a s) n -> a p (s n)", a=2, s=2)[1])
 
+        filler = consts.tile([P, PACK * P], BF16, align_bytes=64)
+        nc.vector.memset(filler[:].bitcast(F32), 1.0)
         bias_row = consts.tile([P, COLUMNS], BF16)
         nc.vector.memset(bias_row[:], 0.0)
+        filler_codes = consts.tile([P, P], U32, align_bytes=64)
+        filler_scales = consts.tile([P, P], U8, align_bytes=64)
+        nc.vector.quantize_mx(
+            out=filler_codes[:].bitcast(FP8X4), scales=filler_scales[:], in_=filler[:]
+        )
+        proj_low = product_banks.tile([P, 2, COLUMNS], F32)
+        proj_high = product_banks.tile([P, 2, COLUMNS], F32)
+
+        def keep_busy(passes):
+            for i in range(passes):
+                nc.tensor.matmul_mx(
+                    out=proj_high[:, 0, :],
+                    lhsT=filler_codes[:].bitcast(FP8X4),
+                    lhsT_scale=filler_scales[:],
+                    rhs=filler_codes[:].bitcast(FP8X4),
+                    rhs_scale=filler_scales[:],
+                    start=True,
+                    stop=True,
+                )
+
         nc.scalar.dma_start(out=bias_row[0:1, :], in_=b.rearrange("h d -> (h d)").unsqueeze(0))
         identity = consts.tile([P, P], F32)
         make_identity(nc, identity[:])
@@ -77,7 +99,7 @@ def tile_graphlayer_s_kernel(tc, H, adj, W, b, out):
             nc.vector.quantize_mx(out=codes[:].bitcast(FP8X4), scales=scales[:], in_=grouped[:])
             return codes, scales
 
-        def quantise_w():
+        def group_w():
             w_grouped = consts.tile([P, FEATURE_PASSES * COLUMNS * PACK], BF16, align_bytes=64)
             for g in range(FEATURE_PASSES):
                 nc.vector.tensor_copy(
@@ -86,6 +108,9 @@ def tile_graphlayer_s_kernel(tc, H, adj, W, b, out):
                     )[:, g],
                     in_=w_raw[:].rearrange("p (h g) (j d) -> p g h d j", g=FEATURE_PASSES, j=PACK)[:, g],
                 )
+            return w_grouped
+
+        def quantise_w(w_grouped):
             w_codes = consts.tile([P, FEATURE_PASSES * COLUMNS], U32, align_bytes=64)
             w_scales = consts.tile([P, FEATURE_PASSES * COLUMNS], U8, align_bytes=64)
             nc.vector.quantize_mx(out=w_codes[:].bitcast(FP8X4), scales=w_scales[:], in_=w_grouped[:])
@@ -95,11 +120,15 @@ def tile_graphlayer_s_kernel(tc, H, adj, W, b, out):
             return slice(s * P, (s + 1) * P)
 
         h_passes = []
+        keep_busy(12)
         for m, h_rows in enumerate(h_tiles[:-1]):
             h_codes, h_scales = quantise(flip_and_empty(h_rows[:], 2), 2)
             h_passes.append([(h_codes, h_scales, section(g)) for g in range(FEATURE_PASSES)])
+            if m == 0:
+                w_grouped = group_w()
             if m == 1:
-                w_codes, w_scales = quantise_w()
+                w_codes, w_scales = quantise_w(w_grouped)
+        keep_busy(8)
         h_passes.append(
             [
                 quantise(flip_and_empty(h_tiles[-1][:, g * K_PASS : (g + 1) * K_PASS], 1), 1) + (section(0),)
@@ -111,8 +140,6 @@ def tile_graphlayer_s_kernel(tc, H, adj, W, b, out):
 
         proj_grouped = consts.tile([P, COLUMNS * PACK], BF16, align_bytes=64)
         proj_to = proj_grouped[:].rearrange("p (c a i) -> p a c i", a=2, i=2)
-        proj_low = product_banks.tile([P, 2, COLUMNS], F32)
-        proj_high = product_banks.tile([P, 2, COLUMNS], F32)
         for a, (proj_half, copy) in enumerate(
             ((proj_low, nc.vector.tensor_copy), (proj_high, nc.scalar.copy))
         ):

@@ -34,17 +34,21 @@ def tile_graphlayer_s_kernel(tc, H, adj, W, b, out):
         product_banks = ctx.enter_context(tc.psum_pool(name="products", bufs=1))
         ctx.enter_context(tc.manual_schedule())
 
-        w_raw = consts.tile([P, HEADS * FEATURE_PASSES, PACK * HEAD_WIDTH], BF16)
+        w_raw = consts.tile([P, FEATURE_PASSES, HEADS, PACK * HEAD_WIDTH], BF16)
         h_tiles = []
         for m in range(ROW_GROUPS):
             h_rows = loads.tile([P, 2 * K_PASS], BF16, tag="rows")
-            nc.sync.dma_start(out=h_rows[:], in_=H.rearrange("(p m) k -> m p k", m=ROW_GROUPS)[m])
+            nc.sync.dma_start(
+                out=h_rows[:],
+                in_=H.rearrange("(u p e) k -> u e p k", u=WORDS, e=PAIR)[m // PAIR, m % PAIR],
+            )
             h_tiles.append(h_rows)
             if m == 2:
-                nc.sync.dma_start(
-                    out=w_raw[:],
-                    in_=W.rearrange("h (g p j) d -> p (h g) (j d)", g=FEATURE_PASSES, j=PACK),
-                )
+                for g in range(FEATURE_PASSES):
+                    nc.sync.dma_start(
+                        out=w_raw[:, g],
+                        in_=W.rearrange("h (g p j) d -> g p h (j d)", g=FEATURE_PASSES, j=PACK)[g],
+                    )
         adj_01 = loads.tile([P, 2 * K_PASS], BF16, tag="rows")
         nc.sync.dma_start(out=adj_01[:], in_=adj.rearrange("(p a s) n -> a p (s n)", a=2, s=2)[0])
         adj_23 = loads.tile([P, 2 * K_PASS], BF16, tag="rows")
@@ -65,7 +69,7 @@ def tile_graphlayer_s_kernel(tc, H, adj, W, b, out):
         def keep_busy(passes):
             for i in range(passes):
                 nc.tensor.matmul_mx(
-                    out=proj_high[:, 0, :],
+                    out=proj_low[:, 0, :],
                     lhsT=filler_codes[:].bitcast(FP8X4),
                     lhsT_scale=filler_scales[:],
                     rhs=filler_codes[:].bitcast(FP8X4),
@@ -80,8 +84,8 @@ def tile_graphlayer_s_kernel(tc, H, adj, W, b, out):
         ones = consts.tile([P, P], BF16)
         nc.vector.memset(ones[:], 1.0)
 
-        def flip_and_empty(rows, sections):
-            words = rows.bitcast(F32).rearrange("r (s p u) -> r s p u", s=sections, u=WORDS)
+        def flip_and_empty(rows, sections, order="r (s p u) -> r s p u"):
+            words = rows.bitcast(F32).rearrange(order, s=sections, u=WORDS)
             flipped = banks.tile([P, sections, WORDS, P], F32, tag="bank")
             for s in range(sections):
                 for u in range(WORDS):
@@ -92,6 +96,8 @@ def tile_graphlayer_s_kernel(tc, H, adj, W, b, out):
                 in_=flipped[:].rearrange("p s u r -> p s r u"),
             )
             return grouped
+
+        adj_order = "r (s u p) -> r s p u"
 
         def quantise(grouped, sections):
             codes = operands.tile([P, sections * P], U32, align_bytes=64, tag="codes")
@@ -106,7 +112,7 @@ def tile_graphlayer_s_kernel(tc, H, adj, W, b, out):
                     out=w_grouped[:].rearrange(
                         "p (g h d j) -> p g h d j", g=FEATURE_PASSES, h=HEADS, j=PACK
                     )[:, g],
-                    in_=w_raw[:].rearrange("p (h g) (j d) -> p g h d j", g=FEATURE_PASSES, j=PACK)[:, g],
+                    in_=w_raw[:, g].rearrange("p h (j d) -> p h d j", j=PACK),
                 )
             return w_grouped
 
@@ -135,7 +141,7 @@ def tile_graphlayer_s_kernel(tc, H, adj, W, b, out):
                 for g in range(FEATURE_PASSES)
             ]
         )
-        adj_01_grouped = flip_and_empty(adj_01[:], 2)
+        adj_01_grouped = flip_and_empty(adj_01[:], 2, adj_order)
         adj_operands = []
 
         proj_grouped = consts.tile([P, COLUMNS * PACK], BF16, align_bytes=64)
@@ -163,12 +169,13 @@ def tile_graphlayer_s_kernel(tc, H, adj, W, b, out):
         nc.vector.quantize_mx(
             out=proj_codes[:].bitcast(FP8X4), scales=proj_scales[:], in_=proj_grouped[:]
         )
-        adj_operands.append(quantise(flip_and_empty(adj_23[:, 0:K_PASS], 1), 1))
-        adj_3_grouped = flip_and_empty(adj_23[:, K_PASS : 2 * K_PASS], 1)
+        adj_operands.append(quantise(flip_and_empty(adj_23[:, 0:K_PASS], 1, adj_order), 1))
+        adj_3_grouped = flip_and_empty(adj_23[:, K_PASS : 2 * K_PASS], 1, adj_order)
         bias_sums = product_banks.tile([P, COLUMNS], F32)
         nc.tensor.matmul(out=bias_sums[:], lhsT=ones[:], rhs=bias_row[:], start=True, stop=True)
+        keep_busy(2)
         bias = consts.tile([P, COLUMNS], F32)
-        nc.vector.tensor_copy(out=bias[:], in_=bias_sums[:])
+        nc.scalar.copy(out=bias[:], in_=bias_sums[:])
         adj_operands.append(quantise(adj_3_grouped, 1))
 
         result = consts.tile([P, ROW_GROUPS, COLUMNS], F32)

@@ -37,11 +37,15 @@ def tile_graphlayer_s_kernel(tc, H, adj, W, b, out):
         w_raw = consts.tile([P, FEATURE_PASSES, HEADS, PACK * HEAD_WIDTH], BF16)
         h_tiles = []
         for m in range(ROW_GROUPS):
-            h_rows = loads.tile([P, 2 * K_PASS], BF16, tag="rows")
-            nc.sync.dma_start(
-                out=h_rows[:],
-                in_=H.rearrange("(u p e) k -> u e p k", u=WORDS, e=PAIR)[m // PAIR, m % PAIR],
-            )
+            h_rows = loads.tile([P, FEATURE_PASSES, K_PASS], BF16, tag="rows")
+            source = H.rearrange("(u p e) (g k) -> u e p g k", u=WORDS, e=PAIR, k=K_PASS)[
+                m // PAIR, m % PAIR
+            ]
+            if m < ROW_GROUPS - 1:
+                nc.sync.dma_start(out=h_rows[:], in_=source)
+            else:
+                for g in range(FEATURE_PASSES):
+                    nc.sync.dma_start(out=h_rows[:, g], in_=source[:, g])
             h_tiles.append(h_rows)
             if m == 2:
                 for g in range(FEATURE_PASSES):
@@ -127,20 +131,23 @@ def tile_graphlayer_s_kernel(tc, H, adj, W, b, out):
 
         h_passes = []
         keep_busy(12)
-        for m, h_rows in enumerate(h_tiles[:-1]):
-            h_codes, h_scales = quantise(flip_and_empty(h_rows[:], 2), 2)
-            h_passes.append([(h_codes, h_scales, section(g)) for g in range(FEATURE_PASSES)])
+        for m, h_rows in enumerate(h_tiles):
+            if m in (0, ROW_GROUPS - 1):
+                h_passes.append(
+                    [
+                        quantise(flip_and_empty(h_rows[:, g], 1), 1) + (section(0),)
+                        for g in range(FEATURE_PASSES)
+                    ]
+                )
+            else:
+                h_codes, h_scales = quantise(flip_and_empty(h_rows[:].rearrange("p g k -> p (g k)"), 2), 2)
+                h_passes.append([(h_codes, h_scales, section(g)) for g in range(FEATURE_PASSES)])
             if m == 0:
                 w_grouped = group_w()
             if m == 1:
                 w_codes, w_scales = quantise_w(w_grouped)
-        keep_busy(8)
-        h_passes.append(
-            [
-                quantise(flip_and_empty(h_tiles[-1][:, g * K_PASS : (g + 1) * K_PASS], 1), 1) + (section(0),)
-                for g in range(FEATURE_PASSES)
-            ]
-        )
+            if m == ROW_GROUPS - 2:
+                keep_busy(8)
         adj_01_grouped = flip_and_empty(adj_01[:], 2, adj_order)
         adj_operands = []
 
@@ -178,29 +185,31 @@ def tile_graphlayer_s_kernel(tc, H, adj, W, b, out):
         nc.scalar.copy(out=bias[:], in_=bias_sums[:])
         adj_operands.append(quantise(adj_3_grouped, 1))
 
+        adj_passes = [
+            (codes, scales, section(s))
+            for (codes, scales), sections in zip(adj_operands, (2, 1, 1))
+            for s in range(sections)
+        ]
         result = consts.tile([P, ROW_GROUPS, COLUMNS], F32)
-        first_group = 0
-        for (adj_codes, adj_scales), sections in zip(adj_operands, (2, 1, 1)):
-            result_sums = banks.tile([P, sections, COLUMNS], F32, tag="bank")
-            for s in range(sections):
-                nc.tensor.matmul_mx(
-                    out=result_sums[:, s, :],
-                    lhsT=adj_codes[:, section(s)].bitcast(FP8X4),
-                    lhsT_scale=adj_scales[:, section(s)],
-                    rhs=proj_codes[:].bitcast(FP8X4),
-                    rhs_scale=proj_scales[:],
-                    start=True,
-                    stop=True,
-                )
-            groups = slice(first_group, first_group + sections)
-            first_group += sections
+        for group in range(ROW_GROUPS):
+            adj_codes, adj_scales, columns = adj_passes[group]
+            result_sums = banks.tile([P, COLUMNS], F32, tag="bank")
+            nc.tensor.matmul_mx(
+                out=result_sums[:],
+                lhsT=adj_codes[:, columns].bitcast(FP8X4),
+                lhsT_scale=adj_scales[:, columns],
+                rhs=proj_codes[:].bitcast(FP8X4),
+                rhs_scale=proj_scales[:],
+                start=True,
+                stop=True,
+            )
             nc.vector.tensor_tensor(
-                out=result[:, groups, :],
+                out=result[:, group, :],
                 in0=result_sums[:],
-                in1=bias[:].unsqueeze(1).to_broadcast([P, sections, COLUMNS]),
+                in1=bias[:],
                 op=mybir.AluOpType.add,
             )
             nc.sync.dma_start(
-                out=out.rearrange("(p m) c -> p m c", m=ROW_GROUPS)[:, groups, :],
-                in_=result[:, groups, :],
+                out=out.rearrange("(p m) c -> m p c", m=ROW_GROUPS)[group],
+                in_=result[:, group, :],
             )

from contextlib import ExitStack

import concourse.mybir as mybir
from concourse.masks import make_identity

BF16 = mybir.dt.bfloat16
F32 = mybir.dt.float32
U32 = mybir.dt.uint32
U8 = mybir.dt.uint8
FP8X4 = mybir.dt.float8_e4m3fn_x4

P = 128
PACK = 4
K_PASS = P * PACK
PAIR = 2
WORDS = PACK // PAIR

NODES, FEATURES, HEADS, HEAD_WIDTH = 512, 1024, 8, 16
COLUMNS = HEADS * HEAD_WIDTH
ROW_GROUPS = NODES // P
FEATURE_PASSES = FEATURES // K_PASS

FLOPS = 2 * NODES * FEATURES * COLUMNS + 2 * NODES * NODES * COLUMNS


def tile_graphlayer_s_kernel(tc, H, adj, W, b, out):
    nc = tc.nc
    with ExitStack() as ctx:
        consts = ctx.enter_context(tc.tile_pool(name="consts", bufs=1))
        loads = ctx.enter_context(tc.tile_pool(name="loads", bufs=8))
        stage = ctx.enter_context(tc.tile_pool(name="stage", bufs=8))
        operands = ctx.enter_context(tc.tile_pool(name="operands", bufs=8))
        banks = ctx.enter_context(tc.psum_pool(name="banks", bufs=5))
        product_banks = ctx.enter_context(tc.psum_pool(name="products", bufs=1))
        ctx.enter_context(tc.manual_schedule())

        w_raw = consts.tile([P, FEATURE_PASSES, HEADS, PACK * HEAD_WIDTH], BF16)
        h_tiles = []
        for m in range(ROW_GROUPS):
            h_rows = loads.tile([P, FEATURE_PASSES, K_PASS], BF16, tag="rows")
            source = H.rearrange("(u p e) (g k) -> u e p g k", u=WORDS, e=PAIR, k=K_PASS)[
                m // PAIR, m % PAIR
            ]
            if m < ROW_GROUPS - 1:
                nc.sync.dma_start(out=h_rows[:], in_=source)
            else:
                for g in range(FEATURE_PASSES):
                    nc.sync.dma_start(out=h_rows[:, g], in_=source[:, g])
            h_tiles.append(h_rows)
            if m == 2:
                for g in range(FEATURE_PASSES):
                    nc.sync.dma_start(
                        out=w_raw[:, g],
                        in_=W.rearrange("h (g p j) d -> g p h (j d)", g=FEATURE_PASSES, j=PACK)[g],
                    )
        adj_01 = loads.tile([P, 2 * K_PASS], BF16, tag="rows")
        nc.sync.dma_start(out=adj_01[:], in_=adj.rearrange("(p a s) n -> a p (s n)", a=2, s=2)[0])
        adj_23 = loads.tile([P, 2 * K_PASS], BF16, tag="rows")
        nc.sync.dma_start(out=adj_23[:], in_=adj.rearrange("(p a s) n -> a p (s n)", a=2, s=2)[1])

        filler = consts.tile([P, PACK * P], BF16, align_bytes=64)
        nc.vector.memset(filler[:].bitcast(F32), 1.0)
        bias_row = consts.tile([P, COLUMNS], BF16)
        nc.vector.memset(bias_row[:], 0.0)
        filler_codes = consts.tile([P, P], U32, align_bytes=64)
        filler_scales = consts.tile([P, P], U8, align_bytes=64)
        nc.vector.quantize_mx(
            out=filler_codes[:].bitcast(FP8X4), scales=filler_scales[:], in_=filler[:]
        )
        proj_low = product_banks.tile([P, 2, COLUMNS], F32)
        proj_high = product_banks.tile([P, 2, COLUMNS], F32)

        def keep_busy(passes):
            for i in range(passes):
                nc.tensor.matmul_mx(
                    out=proj_low[:, 0, :],
                    lhsT=filler_codes[:].bitcast(FP8X4),
                    lhsT_scale=filler_scales[:],
                    rhs=filler_codes[:].bitcast(FP8X4),
                    rhs_scale=filler_scales[:],
                    start=True,
                    stop=True,
                )

        nc.scalar.dma_start(out=bias_row[0:1, :], in_=b.rearrange("h d -> (h d)").unsqueeze(0))
        identity = consts.tile([P, P], F32)
        make_identity(nc, identity[:])
        ones = consts.tile([P, P], BF16)
        nc.vector.memset(ones[:], 1.0)

        def flip_and_empty(rows, sections, order="r (s p u) -> r s p u"):
            words = rows.bitcast(F32).rearrange(order, s=sections, u=WORDS)
            flipped = banks.tile([P, sections, WORDS, P], F32, tag="bank")
            for s in range(sections):
                for u in range(WORDS):
                    nc.tensor.transpose(flipped[:, s, u, :], words[:, s, :, u], identity[:])
            grouped = stage.tile([P, sections * P * PACK], BF16, align_bytes=64, tag="grouped")
            nc.scalar.copy(
                out=grouped[:].bitcast(F32).rearrange("p (s r u) -> p s r u", s=sections, u=WORDS),
                in_=flipped[:].rearrange("p s u r -> p s r u"),
            )
            return grouped

        adj_order = "r (s u p) -> r s p u"

        def quantise(grouped, sections):
            codes = operands.tile([P, sections * P], U32, align_bytes=64, tag="codes")
            scales = operands.tile([P, sections * P], U8, align_bytes=64, tag="scales")
            nc.vector.quantize_mx(out=codes[:].bitcast(FP8X4), scales=scales[:], in_=grouped[:])
            return codes, scales

        def group_w():
            w_grouped = consts.tile([P, FEATURE_PASSES * COLUMNS * PACK], BF16, align_bytes=64)
            for g in range(FEATURE_PASSES):
                nc.vector.tensor_copy(
                    out=w_grouped[:].rearrange(
                        "p (g h d j) -> p g h d j", g=FEATURE_PASSES, h=HEADS, j=PACK
                    )[:, g],
                    in_=w_raw[:, g].rearrange("p h (j d) -> p h d j", j=PACK),
                )
            return w_grouped

        def quantise_w(w_grouped):
            w_codes = consts.tile([P, FEATURE_PASSES * COLUMNS], U32, align_bytes=64)
            w_scales = consts.tile([P, FEATURE_PASSES * COLUMNS], U8, align_bytes=64)
            nc.vector.quantize_mx(out=w_codes[:].bitcast(FP8X4), scales=w_scales[:], in_=w_grouped[:])
            return w_codes, w_scales

        def section(s):
            return slice(s * P, (s + 1) * P)

        h_passes = []
        keep_busy(12)
        for m, h_rows in enumerate(h_tiles):
            if m in (0, ROW_GROUPS - 1):
                h_passes.append(
                    [
                        quantise(flip_and_empty(h_rows[:, g], 1), 1) + (section(0),)
                        for g in range(FEATURE_PASSES)
                    ]
                )
            else:
                h_codes, h_scales = quantise(flip_and_empty(h_rows[:].rearrange("p g k -> p (g k)"), 2), 2)
                h_passes.append([(h_codes, h_scales, section(g)) for g in range(FEATURE_PASSES)])
            if m == 0:
                w_grouped = group_w()
            if m == 1:
                w_codes, w_scales = quantise_w(w_grouped)
            if m == ROW_GROUPS - 2:
                keep_busy(8)
        adj_01_grouped = flip_and_empty(adj_01[:], 2, adj_order)
        adj_operands = []

        proj_grouped = consts.tile([P, COLUMNS * PACK], BF16, align_bytes=64)
        proj_to = proj_grouped[:].rearrange("p (c a i) -> p a c i", a=2, i=2)
        for a, (proj_half, copy) in enumerate(
            ((proj_low, nc.vector.tensor_copy), (proj_high, nc.scalar.copy))
        ):
            for i in range(2):
                for g in range(FEATURE_PASSES):
                    h_codes, h_scales, columns = h_passes[2 * a + i][g]
                    nc.tensor.matmul_mx(
                        out=proj_half[:, i, :],
                        lhsT=h_codes[:, columns].bitcast(FP8X4),
                        lhsT_scale=h_scales[:, columns],
                        rhs=w_codes[:, section(g)].bitcast(FP8X4),
                        rhs_scale=w_scales[:, section(g)],
                        start=(g == 0),
                        stop=(g == FEATURE_PASSES - 1),
                    )
            copy(out=proj_to[:, a], in_=proj_half[:].rearrange("p i c -> p c i"))
            if a == 0:
                adj_operands.append(quantise(adj_01_grouped, 2))
        proj_codes = consts.tile([P, COLUMNS], U32, align_bytes=64)
        proj_scales = consts.tile([P, COLUMNS], U8, align_bytes=64)
        nc.vector.quantize_mx(
            out=proj_codes[:].bitcast(FP8X4), scales=proj_scales[:], in_=proj_grouped[:]
        )
        adj_operands.append(quantise(flip_and_empty(adj_23[:, 0:K_PASS], 1, adj_order), 1))
        adj_3_grouped = flip_and_empty(adj_23[:, K_PASS : 2 * K_PASS], 1, adj_order)
        bias_sums = product_banks.tile([P, COLUMNS], F32)
        nc.tensor.matmul(out=bias_sums[:], lhsT=ones[:], rhs=bias_row[:], start=True, stop=True)
        keep_busy(2)
        bias = consts.tile([P, COLUMNS], F32)
        nc.scalar.copy(out=bias[:], in_=bias_sums[:])
        adj_operands.append(quantise(adj_3_grouped, 1))

        adj_passes = [
            (codes, scales, section(s))
            for (codes, scales), sections in zip(adj_operands, (2, 1, 1))
            for s in range(sections)
        ]
        result = consts.tile([P, ROW_GROUPS, COLUMNS], F32)
        for group in range(ROW_GROUPS):
            adj_codes, adj_scales, columns = adj_passes[group]
            result_sums = banks.tile([P, COLUMNS], F32, tag="bank")
            nc.tensor.matmul_mx(
                out=result_sums[:],
                lhsT=adj_codes[:, columns].bitcast(FP8X4),
                lhsT_scale=adj_scales[:, columns],
                rhs=proj_codes[:].bitcast(FP8X4),
                rhs_scale=proj_scales[:],
                start=True,
                stop=True,
            )
            nc.vector.tensor_tensor(
                out=result[:, group, :],
                in0=result_sums[:],
                in1=bias[:],
                op=mybir.AluOpType.add,
            )
            nc.sync.dma_start(
                out=out.rearrange("(p m) c -> m p c", m=ROW_GROUPS)[group],
                in_=result[:, group, :],
            )
